import numpy as np
import ml_dtypes


def mxq(x, axis, fmt="e4m3"):
    dtype, down = {"e4m3": (ml_dtypes.float8_e4m3fn, 7), "e5m2": (ml_dtypes.float8_e5m2, 14)}[fmt]
    v = np.moveaxis(np.asarray(x, np.float32).astype(ml_dtypes.bfloat16).astype(np.float64), axis, -1)
    blocks = v.reshape(v.shape[:-1] + (-1, 32))
    amax = np.abs(blocks).max(-1, keepdims=True)
    byte = np.maximum(np.where(amax > 0, np.frexp(amax)[1] - 1 + 127, 0) - down, 1)
    scale = np.exp2(byte - 127.0)
    codes = (blocks / scale).astype(np.float32).astype(dtype).astype(np.float64)
    return np.moveaxis((codes * scale).reshape(v.shape), -1, axis)


WIDE = False


def mx_kscale(k):
    if not WIDE:
        return np.ones(k)
    levels = np.array([10, -10, 5, -5, 0])
    a = np.random.permutation(np.resize(levels, k // 512 * 4)).reshape(k // 512, 4)
    idx = np.arange(k)
    return np.exp2(a[idx // 512, idx % 128 // 32])


BF16 = ml_dtypes.bfloat16


def bf(x):
    return np.asarray(x, np.float32).astype(BF16)


def f64(x):
    return np.asarray(x).astype(np.float64)


B, L, D, CH, S, R, NL = 1, 4096, 1024, 1, 8, 128, 4
EPS = 1e-6


def rmsnorm(v, w):
    return v / np.sqrt(np.mean(v * v, axis=-1, keepdims=True) + EPS) * w


def setup_inputs():
    n = np.random.standard_normal
    t = mx_kscale(CH * D)
    return {"y": bf(n((B, L, CH * D)) * 0.9 * t),
            "x": bf(n((B, L, D))),
            "step_emb": bf(n(D) * 0.3),
            "out_proj_w": bf(n((D, CH * D)) / np.sqrt(CH * D) / t[None, :]),
            "mixer_norm_w": bf(1.0 + 0.1 * n(D)),
            "loop_norm_w": bf(1.0 + 0.1 * n(D))}


def reference(y, x, step_emb, out_proj_w, mixer_norm_w, loop_norm_w):
    h = f64(x) + f64(step_emb)
    out = rmsnorm(mxq(f64(y), 2, "e4m3") @ mxq(f64(out_proj_w), 1, "e4m3").T, f64(mixer_norm_w))
    return rmsnorm(h + out, f64(loop_norm_w))

@@ -1,0 +1,305 @@
+from contextlib import ExitStack
+
+import concourse.mybir as mybir
+from concourse.masks import make_identity
+
+F32 = mybir.dt.float32
+BF16 = mybir.dt.bfloat16
+U32 = mybir.dt.uint32
+U8 = mybir.dt.uint8
+FP8X4 = mybir.dt.float8_e4m3fn_x4
+ACT = mybir.ActivationFunctionType
+ALU = mybir.AluOpType
+
+P = 128
+TOKENS = 4096
+D = 1024
+EPS = 1e-6
+PACK = 4
+K_PASS = P * PACK
+PASSES = D // K_PASS
+BANK = 512
+HALVES = D // BANK
+PAIRS = 2
+BLOCKS = D // PAIRS // P
+GROUP = 4
+N_TILES = TOKENS // P
+N_GROUPS = N_TILES // GROUP
+W_TILES = D // P
+GPSIMD_COLS = 256
+
+FLIP_AHEAD = 5
+RESIDUAL_AHEAD = 4
+QUANTISE_AHEAD = 3
+MULTIPLY_AHEAD = 2
+NORM_P_AHEAD = 1
+SUM_Z_BEHIND = 2
+FINISH_BEHIND = 3
+LOAD_GROUPS_AHEAD = 2
+
+FLOPS = 2 * TOKENS * D * D
+
+
+def tile_recursivemamba130m_pb_t_kernel(
+    tc, y, x, step_emb, out_proj_w, mixer_norm_w, loop_norm_w, out
+):
+    nc = tc.nc
+    y_groups = y.flatten_outer_dims().rearrange("(g p t) k -> g p t k", p=P, t=GROUP)
+    x_groups = x.flatten_outer_dims().rearrange("(g p t) c -> g p t c", p=P, t=GROUP)
+    out_groups = out.flatten_outer_dims().rearrange("(g p t) c -> g p t c", p=P, t=GROUP)
+
+    with ExitStack() as stack:
+        stack.enter_context(tc.manual_schedule())
+        const = stack.enter_context(tc.tile_pool(name="const", bufs=1))
+        loads = stack.enter_context(tc.tile_pool(name="loads", bufs=LOAD_GROUPS_AHEAD + 1))
+        operand = stack.enter_context(tc.tile_pool(name="operand", bufs=4))
+        work = stack.enter_context(tc.tile_pool(name="work", bufs=3))
+        unread = stack.enter_context(tc.tile_pool(name="unread", bufs=3))
+        small = stack.enter_context(tc.tile_pool(name="small", bufs=4))
+        const_psum = stack.enter_context(tc.psum_pool(name="const_psum", bufs=1))
+        flip_psum = stack.enter_context(tc.psum_pool(name="flip_psum", bufs=2))
+        acc_psum = stack.enter_context(tc.psum_pool(name="acc_psum", bufs=2 * HALVES))
+
+        w_rows = const.tile([P, W_TILES, D], BF16)
+        w_view = out_proj_w.rearrange("(j p) k -> p j k", p=P)
+        for j in range(0, W_TILES, 2):
+            nc.sync.dma_start(out=w_rows[:, j : j + 2, :], in_=w_view[:, j : j + 2, :])
+
+        y_tiles = {}
+        x_tiles = {}
+
+        def load_group(g, pieces):
+            y_rows = loads.tile([P, GROUP, D], BF16)
+            x_rows = loads.tile([P, GROUP, D], BF16)
+            step = GROUP // pieces
+            for t in range(0, GROUP, step):
+                nc.sync.dma_start(out=y_rows[:, t : t + step, :], in_=y_groups[g][:, t : t + step, :])
+                nc.sync.dma_start(out=x_rows[:, t : t + step, :], in_=x_groups[g][:, t : t + step, :])
+            for t in range(GROUP):
+                y_tiles[g * GROUP + t] = y_rows[:, t, :]
+                x_tiles[g * GROUP + t] = x_rows[:, t, :]
+
+        load_group(0, GROUP)
+        for g in range(1, LOAD_GROUPS_AHEAD):
+            load_group(g, 1)
+
+        vec_rows = const.tile([P, 3, D], BF16)
+        nc.vector.memset(vec_rows[:], 0.0)
+        nc.scalar.dma_start(out=vec_rows[0:1, 0, :], in_=step_emb.unsqueeze(0))
+        nc.scalar.dma_start(out=vec_rows[0:1, 1, :], in_=mixer_norm_w.unsqueeze(0))
+        nc.scalar.dma_start(out=vec_rows[0:1, 2, :], in_=loop_norm_w.unsqueeze(0))
+        eps_col = const.tile([P, 1], F32)
+        nc.vector.memset(eps_col[:], EPS)
+        table_warmer = const.tile([P, 1], F32)
+        nc.scalar.activation(out=table_warmer[:], in_=eps_col[:], func=ACT.Abs_reciprocal_sqrt)
+        ones = const.tile([P, P], BF16)
+        nc.vector.memset(ones[:], 1.0)
+        ident = const.tile([P, P], F32)
+        make_identity(nc, ident[:])
+
+        emb_bank = const_psum.tile([P, D], BF16)
+        gain1_bank = flip_psum.tile([P, D], BF16, tag="flip")
+        gain2_bank = const_psum.tile([P, D], BF16)
+        spread_banks = [emb_bank, gain1_bank, gain2_bank]
+        gain1 = const.tile([P, D], BF16)
+        emb_head = const.tile([P, GPSIMD_COLS], BF16)
+
+        def spread(v):
+            for h in range(HALVES):
+                cols = slice(h * BANK, (h + 1) * BANK)
+                nc.tensor.matmul(
+                    out=spread_banks[v][:, cols], lhsT=ones[:], rhs=vec_rows[:, v, cols],
+                    start=True, stop=True,
+                )
+
+        def flip(rows, bank):
+            words = rows.bitcast(F32)
+            for b in range(BLOCKS):
+                nc.tensor.transpose(bank[:, b, :], words[:, b * P : (b + 1) * P], ident[:])
+
+        def by_pass(bank):
+            return bank[:].rearrange("q (c u) r -> q c r u", c=PASSES, u=PAIRS)
+
+        w_grouped = const.tile([P, PASSES, D * PACK], BF16, align_bytes=64)
+        w_grouped_words = w_grouped[:].bitcast(F32).rearrange("q c (n u) -> q c n u", u=PAIRS)
+        w_codes = const.tile([P, PASSES, D], U32, align_bytes=64)
+        w_scales = const.tile([P, PASSES, D], U8, align_bytes=64)
+
+        def quantise_w(j):
+            for c in range(PASSES):
+                nc.vector.quantize_mx(
+                    out=w_codes[:, c, j * P : (j + 1) * P].bitcast(FP8X4),
+                    scales=w_scales[:, c, j * P : (j + 1) * P],
+                    in_=w_grouped[:, c, j * P * PACK : (j + 1) * P * PACK],
+                )
+
+        for j in range(W_TILES):
+            w_bank = acc_psum.tile([P, BLOCKS, P], F32, tag="acc")
+            flip(w_rows[:, j, :], w_bank)
+            target = w_grouped_words[:, :, j * P : (j + 1) * P, :]
+            if j % 2 == 0:
+                nc.scalar.copy(out=target, in_=by_pass(w_bank))
+            else:
+                nc.vector.tensor_copy(out=target, in_=by_pass(w_bank))
+            if j % 2 == 1 and j // 2 < len(spread_banks):
+                spread(j // 2)
+            if j >= 1:
+                quantise_w(j - 1)
+        quantise_w(W_TILES - 1)
+        nc.scalar.copy(out=gain1[:], in_=gain1_bank[:])
+        nc.vector.tensor_copy(out=emb_head[:], in_=emb_bank[:, :GPSIMD_COLS])
+
+        flipped_of = {}
+        grouped_of = {}
+        codes_of = {}
+        acc_of = {}
+        sums_of = {}
+        part_of = {}
+        inv1_of = {}
+        branch_of = {}
+        resid_of = {}
+        z_of = {}
+        total_of = {}
+        inv2_of = {}
+
+        def transpose_tile(i):
+            y_bank = flip_psum.tile([P, BLOCKS, P], F32, tag="flip")
+            flip(y_tiles[i], y_bank)
+            flipped_of[i] = y_bank
+
+        def regroup_tile(i):
+            grouped = operand.tile([P, D], BF16, align_bytes=64)
+            nc.scalar.copy(
+                out=grouped[:].bitcast(F32).rearrange("q (c r u) -> q c r u", c=PASSES, u=PAIRS),
+                in_=by_pass(flipped_of[i]),
+            )
+            grouped_of[i] = grouped
+
+        def quantise_tile(i):
+            codes = operand.tile([P, PASSES * P], U32, align_bytes=64)
+            scales = operand.tile([P, PASSES * P], U8, align_bytes=64)
+            nc.vector.quantize_mx(
+                out=codes[:].bitcast(FP8X4), scales=scales[:], in_=grouped_of[i][:]
+            )
+            codes_of[i] = (codes, scales)
+
+        def multiply_tile(i):
+            codes, scales = codes_of[i]
+            banks = []
+            for h in range(HALVES):
+                acc = acc_psum.tile([P, BANK], F32, tag="acc")
+                for c in range(PASSES):
+                    nc.tensor.matmul_mx(
+                        out=acc[:],
+                        lhsT=codes[:, c * P : (c + 1) * P].bitcast(FP8X4),
+                        lhsT_scale=scales[:, c * P : (c + 1) * P],
+                        rhs=w_codes[:, c, h * BANK : (h + 1) * BANK].bitcast(FP8X4),
+                        rhs_scale=w_scales[:, c, h * BANK : (h + 1) * BANK],
+                        start=(c == 0),
+                        stop=(c == PASSES - 1),
+                    )
+                banks.append(acc)
+            acc_of[i] = banks
+
+        def sum_p(i, h):
+            if h == 0:
+                sums = small.tile([P, HALVES], F32)
+                sums_of[i] = sums
+            squares = unread.tile([P, BANK], F32)
+            nc.scalar.activation(
+                out=squares[:], in_=acc_of[i][h][:], func=ACT.Square,
+                accum_out=sums_of[i][:, h : h + 1],
+            )
+
+        def part_p(i):
+            part = small.tile([P, 1], F32)
+            nc.scalar.activation(
+                out=part[:], in_=sums_of[i][:, 0:1], func=ACT.Identity, scale=1.0 / D,
+                bias=eps_col[:],
+            )
+            part_of[i] = part
+
+        def root_p(i):
+            inv1 = small.tile([P, 1], F32)
+            nc.scalar.activation(
+                out=inv1[:], in_=sums_of[i][:, 1:2], func=ACT.Abs_reciprocal_sqrt, scale=1.0 / D,
+                bias=part_of[i][:],
+            )
+            inv1_of[i] = inv1
+
+        def branch_tile(i):
+            branch = work.tile([P, D], F32)
+            for h in range(HALVES):
+                cols = slice(h * BANK, (h + 1) * BANK)
+                nc.vector.scalar_tensor_tensor(
+                    out=branch[:, cols], in0=acc_of[i][h][:], scalar=inv1_of[i][:],
+                    in1=gain1[:, cols], op0=ALU.mult, op1=ALU.mult,
+                )
+            branch_of[i] = branch
+
+        def residual_tile(i):
+            resid = work.tile([P, D], F32, bufs=RESIDUAL_AHEAD + 3)
+            nc.gpsimd.tensor_tensor(
+                out=resid[:, :GPSIMD_COLS], in0=x_tiles[i][:, :GPSIMD_COLS], in1=emb_head[:],
+                op=ALU.add,
+            )
+            nc.vector.tensor_tensor(
+                out=resid[:, GPSIMD_COLS:], in0=x_tiles[i][:, GPSIMD_COLS:],
+                in1=emb_bank[:, GPSIMD_COLS:], op=ALU.add,
+            )
+            resid_of[i] = resid
+
+        def add_tile(i):
+            z = work.tile([P, D], F32, bufs=FINISH_BEHIND + 2)
+            nc.gpsimd.tensor_tensor(out=z[:], in0=branch_of[i][:], in1=resid_of[i][:], op=ALU.add)
+            z_of[i] = z
+
+        def sum_z(i):
+            total = small.tile([P, 1], F32)
+            squares2 = unread.tile([P, D], F32, bufs=2)
+            nc.scalar.activation(
+                out=squares2[:], in_=z_of[i][:], func=ACT.Square, accum_out=total[:]
+            )
+            total_of[i] = total
+
+        def root_z(i):
+            inv2 = small.tile([P, 1], F32)
+            nc.scalar.activation(
+                out=inv2[:], in_=total_of[i][:], func=ACT.Abs_reciprocal_sqrt, scale=1.0 / D,
+                bias=eps_col[:],
+            )
+            inv2_of[i] = inv2
+
+        def finish_tile(i):
+            result = work.tile([P, D], F32, bufs=4)
+            nc.vector.scalar_tensor_tensor(
+                out=result[:], in0=z_of[i][:], scalar=inv2_of[i][:], in1=gain2_bank[:],
+                op0=ALU.mult, op1=ALU.mult,
+            )
+            nc.sync.dma_start(out=out_groups[i // GROUP][:, i % GROUP, :], in_=result[:])
+
+        def live(i):
+            return 0 <= i < N_TILES
+
+        def at(stage, i, *more):
+            if live(i):
+                stage(i, *more)
+
+        for s in range(-FLIP_AHEAD, N_TILES + FINISH_BEHIND):
+            first_x = s + RESIDUAL_AHEAD
+            if first_x % GROUP == 0 and 0 <= first_x // GROUP < N_GROUPS - LOAD_GROUPS_AHEAD:
+                load_group(first_x // GROUP + LOAD_GROUPS_AHEAD, 1)
+            at(transpose_tile, s + FLIP_AHEAD)
+            at(branch_tile, s)
+            at(add_tile, s)
+            at(quantise_tile, s + QUANTISE_AHEAD)
+            at(multiply_tile, s + MULTIPLY_AHEAD)
+            at(residual_tile, s + RESIDUAL_AHEAD)
+            at(sum_p, s + NORM_P_AHEAD, 0)
+            at(root_z, s - FINISH_BEHIND)
+            at(sum_p, s + NORM_P_AHEAD, 1)
+            at(part_p, s + NORM_P_AHEAD)
+            at(sum_z, s - SUM_Z_BEHIND)
+            at(root_p, s + NORM_P_AHEAD)
+            at(regroup_tile, s + FLIP_AHEAD)
+            at(finish_tile, s - FINISH_BEHIND)

@@ -26,11 +26,12 @@ GROUP = 4
 N_TILES = TOKENS // P
 N_GROUPS = N_TILES // GROUP
 W_TILES = D // P
-GPSIMD_COLS = 256
+GPSIMD_COLS = 192
 
 FLIP_AHEAD = 5
-RESIDUAL_AHEAD = 4
+REGROUP_AHEAD = 4
 QUANTISE_AHEAD = 3
+RESIDUAL_AHEAD = 3
 MULTIPLY_AHEAD = 2
 NORM_P_AHEAD = 1
 SUM_Z_BEHIND = 2
@@ -60,6 +61,13 @@ def tile_recursivemamba130m_pb_t_kernel(
         flip_psum = stack.enter_context(tc.psum_pool(name="flip_psum", bufs=2))
         acc_psum = stack.enter_context(tc.psum_pool(name="acc_psum", bufs=2 * HALVES))
 
+        vec_rows = []
+        for vector in (step_emb, mixer_norm_w, loop_norm_w):
+            rows = const.tile([P, D], BF16, name="vec_rows%d" % len(vec_rows))
+            nc.vector.memset(rows[:], 0.0)
+            nc.scalar.dma_start(out=rows[0:1, :], in_=vector.unsqueeze(0))
+            vec_rows.append(rows)
+
         w_rows = const.tile([P, W_TILES, D], BF16)
         w_view = out_proj_w.rearrange("(j p) k -> p j k", p=P)
         for j in range(0, W_TILES, 2):
@@ -74,6 +82,7 @@ def tile_recursivemamba130m_pb_t_kernel(
             step = GROUP // pieces
             for t in range(0, GROUP, step):
                 nc.sync.dma_start(out=y_rows[:, t : t + step, :], in_=y_groups[g][:, t : t + step, :])
+            for t in range(0, GROUP, step):
                 nc.sync.dma_start(out=x_rows[:, t : t + step, :], in_=x_groups[g][:, t : t + step, :])
             for t in range(GROUP):
                 y_tiles[g * GROUP + t] = y_rows[:, t, :]
@@ -83,11 +92,6 @@ def tile_recursivemamba130m_pb_t_kernel(
         for g in range(1, LOAD_GROUPS_AHEAD):
             load_group(g, 1)
 
-        vec_rows = const.tile([P, 3, D], BF16)
-        nc.vector.memset(vec_rows[:], 0.0)
-        nc.scalar.dma_start(out=vec_rows[0:1, 0, :], in_=step_emb.unsqueeze(0))
-        nc.scalar.dma_start(out=vec_rows[0:1, 1, :], in_=mixer_norm_w.unsqueeze(0))
-        nc.scalar.dma_start(out=vec_rows[0:1, 2, :], in_=loop_norm_w.unsqueeze(0))
         eps_col = const.tile([P, 1], F32)
         nc.vector.memset(eps_col[:], EPS)
         table_warmer = const.tile([P, 1], F32)
@@ -101,6 +105,7 @@ def tile_recursivemamba130m_pb_t_kernel(
         gain1_bank = flip_psum.tile([P, D], BF16, tag="flip")
         gain2_bank = const_psum.tile([P, D], BF16)
         spread_banks = [emb_bank, gain1_bank, gain2_bank]
+        EMB, GAIN1, GAIN2 = 0, 1, 2
         gain1 = const.tile([P, D], BF16)
         emb_head = const.tile([P, GPSIMD_COLS], BF16)
 
@@ -108,7 +113,7 @@ def tile_recursivemamba130m_pb_t_kernel(
             for h in range(HALVES):
                 cols = slice(h * BANK, (h + 1) * BANK)
                 nc.tensor.matmul(
-                    out=spread_banks[v][:, cols], lhsT=ones[:], rhs=vec_rows[:, v, cols],
+                    out=spread_banks[v][:, cols], lhsT=ones[:], rhs=vec_rows[v][:, cols],
                     start=True, stop=True,
                 )
 
@@ -141,8 +146,10 @@ def tile_recursivemamba130m_pb_t_kernel(
                 nc.scalar.copy(out=target, in_=by_pass(w_bank))
             else:
                 nc.vector.tensor_copy(out=target, in_=by_pass(w_bank))
-            if j % 2 == 1 and j // 2 < len(spread_banks):
-                spread(j // 2)
+            if j == 1:
+                spread(EMB)
+            if j == 3:
+                spread(GAIN1)
             if j >= 1:
                 quantise_w(j - 1)
         quantise_w(W_TILES - 1)
@@ -251,7 +258,8 @@ def tile_recursivemamba130m_pb_t_kernel(
 
         def add_tile(i):
             z = work.tile([P, D], F32, bufs=FINISH_BEHIND + 2)
-            nc.gpsimd.tensor_tensor(out=z[:], in0=branch_of[i][:], in1=resid_of[i][:], op=ALU.add)
+            engine = nc.vector if i == N_TILES - 1 else nc.gpsimd
+            engine.tensor_tensor(out=z[:], in0=branch_of[i][:], in1=resid_of[i][:], op=ALU.add)
             z_of[i] = z
 
         def sum_z(i):
@@ -289,17 +297,19 @@ def tile_recursivemamba130m_pb_t_kernel(
             first_x = s + RESIDUAL_AHEAD
             if first_x % GROUP == 0 and 0 <= first_x // GROUP < N_GROUPS - LOAD_GROUPS_AHEAD:
                 load_group(first_x // GROUP + LOAD_GROUPS_AHEAD, 1)
-            at(transpose_tile, s + FLIP_AHEAD)
             at(branch_tile, s)
             at(add_tile, s)
             at(quantise_tile, s + QUANTISE_AHEAD)
-            at(multiply_tile, s + MULTIPLY_AHEAD)
             at(residual_tile, s + RESIDUAL_AHEAD)
+            at(multiply_tile, s + MULTIPLY_AHEAD)
+            if s + MULTIPLY_AHEAD == 0:
+                spread(GAIN2)
+            at(transpose_tile, s + FLIP_AHEAD)
             at(sum_p, s + NORM_P_AHEAD, 0)
             at(root_z, s - FINISH_BEHIND)
             at(sum_p, s + NORM_P_AHEAD, 1)
             at(part_p, s + NORM_P_AHEAD)
             at(sum_z, s - SUM_Z_BEHIND)
             at(root_p, s + NORM_P_AHEAD)
-            at(regroup_tile, s + FLIP_AHEAD)
+            at(regroup_tile, s + REGROUP_AHEAD)
             at(finish_tile, s - FINISH_BEHIND)

@@ -26,7 +26,7 @@ GROUP = 4
 N_TILES = TOKENS // P
 N_GROUPS = N_TILES // GROUP
 W_TILES = D // P
-GPSIMD_COLS = 192
+GPSIMD_COLS = 320
 
 FLIP_AHEAD = 5
 REGROUP_AHEAD = 4

from contextlib import ExitStack

import concourse.mybir as mybir
from concourse.masks import make_identity

F32 = mybir.dt.float32
BF16 = mybir.dt.bfloat16
U32 = mybir.dt.uint32
U8 = mybir.dt.uint8
FP8X4 = mybir.dt.float8_e4m3fn_x4
ACT = mybir.ActivationFunctionType
ALU = mybir.AluOpType

P = 128
TOKENS = 4096
D = 1024
EPS = 1e-6
PACK = 4
K_PASS = P * PACK
PASSES = D // K_PASS
BANK = 512
HALVES = D // BANK
PAIRS = 2
BLOCKS = D // PAIRS // P
GROUP = 4
N_TILES = TOKENS // P
N_GROUPS = N_TILES // GROUP
W_TILES = D // P
GPSIMD_COLS = 320

FLIP_AHEAD = 5
REGROUP_AHEAD = 4
QUANTISE_AHEAD = 3
RESIDUAL_AHEAD = 3
MULTIPLY_AHEAD = 2
NORM_P_AHEAD = 1
SUM_Z_BEHIND = 2
FINISH_BEHIND = 3
LOAD_GROUPS_AHEAD = 2

FLOPS = 2 * TOKENS * D * D


def tile_recursivemamba130m_pb_t_kernel(
    tc, y, x, step_emb, out_proj_w, mixer_norm_w, loop_norm_w, out
):
    nc = tc.nc
    y_groups = y.flatten_outer_dims().rearrange("(g p t) k -> g p t k", p=P, t=GROUP)
    x_groups = x.flatten_outer_dims().rearrange("(g p t) c -> g p t c", p=P, t=GROUP)
    out_groups = out.flatten_outer_dims().rearrange("(g p t) c -> g p t c", p=P, t=GROUP)

    with ExitStack() as stack:
        stack.enter_context(tc.manual_schedule())
        const = stack.enter_context(tc.tile_pool(name="const", bufs=1))
        loads = stack.enter_context(tc.tile_pool(name="loads", bufs=LOAD_GROUPS_AHEAD + 1))
        operand = stack.enter_context(tc.tile_pool(name="operand", bufs=4))
        work = stack.enter_context(tc.tile_pool(name="work", bufs=3))
        unread = stack.enter_context(tc.tile_pool(name="unread", bufs=3))
        small = stack.enter_context(tc.tile_pool(name="small", bufs=4))
        const_psum = stack.enter_context(tc.psum_pool(name="const_psum", bufs=1))
        flip_psum = stack.enter_context(tc.psum_pool(name="flip_psum", bufs=2))
        acc_psum = stack.enter_context(tc.psum_pool(name="acc_psum", bufs=2 * HALVES))

        vec_rows = []
        for vector in (step_emb, mixer_norm_w, loop_norm_w):
            rows = const.tile([P, D], BF16, name="vec_rows%d" % len(vec_rows))
            nc.vector.memset(rows[:], 0.0)
            nc.scalar.dma_start(out=rows[0:1, :], in_=vector.unsqueeze(0))
            vec_rows.append(rows)

        w_rows = const.tile([P, W_TILES, D], BF16)
        w_view = out_proj_w.rearrange("(j p) k -> p j k", p=P)
        for j in range(0, W_TILES, 2):
            nc.sync.dma_start(out=w_rows[:, j : j + 2, :], in_=w_view[:, j : j + 2, :])

        y_tiles = {}
        x_tiles = {}

        def load_group(g, pieces):
            y_rows = loads.tile([P, GROUP, D], BF16)
            x_rows = loads.tile([P, GROUP, D], BF16)
            step = GROUP // pieces
            for t in range(0, GROUP, step):
                nc.sync.dma_start(out=y_rows[:, t : t + step, :], in_=y_groups[g][:, t : t + step, :])
            for t in range(0, GROUP, step):
                nc.sync.dma_start(out=x_rows[:, t : t + step, :], in_=x_groups[g][:, t : t + step, :])
            for t in range(GROUP):
                y_tiles[g * GROUP + t] = y_rows[:, t, :]
                x_tiles[g * GROUP + t] = x_rows[:, t, :]

        load_group(0, GROUP)
        for g in range(1, LOAD_GROUPS_AHEAD):
            load_group(g, 1)

        eps_col = const.tile([P, 1], F32)
        nc.vector.memset(eps_col[:], EPS)
        table_warmer = const.tile([P, 1], F32)
        nc.scalar.activation(out=table_warmer[:], in_=eps_col[:], func=ACT.Abs_reciprocal_sqrt)
        ones = const.tile([P, P], BF16)
        nc.vector.memset(ones[:], 1.0)
        ident = const.tile([P, P], F32)
        make_identity(nc, ident[:])

        emb_bank = const_psum.tile([P, D], BF16)
        gain1_bank = flip_psum.tile([P, D], BF16, tag="flip")
        gain2_bank = const_psum.tile([P, D], BF16)
        spread_banks = [emb_bank, gain1_bank, gain2_bank]
        EMB, GAIN1, GAIN2 = 0, 1, 2
        gain1 = const.tile([P, D], BF16)
        emb_head = const.tile([P, GPSIMD_COLS], BF16)

        def spread(v):
            for h in range(HALVES):
                cols = slice(h * BANK, (h + 1) * BANK)
                nc.tensor.matmul(
                    out=spread_banks[v][:, cols], lhsT=ones[:], rhs=vec_rows[v][:, cols],
                    start=True, stop=True,
                )

        def flip(rows, bank):
            words = rows.bitcast(F32)
            for b in range(BLOCKS):
                nc.tensor.transpose(bank[:, b, :], words[:, b * P : (b + 1) * P], ident[:])

        def by_pass(bank):
            return bank[:].rearrange("q (c u) r -> q c r u", c=PASSES, u=PAIRS)

        w_grouped = const.tile([P, PASSES, D * PACK], BF16, align_bytes=64)
        w_grouped_words = w_grouped[:].bitcast(F32).rearrange("q c (n u) -> q c n u", u=PAIRS)
        w_codes = const.tile([P, PASSES, D], U32, align_bytes=64)
        w_scales = const.tile([P, PASSES, D], U8, align_bytes=64)

        def quantise_w(j):
            for c in range(PASSES):
                nc.vector.quantize_mx(
                    out=w_codes[:, c, j * P : (j + 1) * P].bitcast(FP8X4),
                    scales=w_scales[:, c, j * P : (j + 1) * P],
                    in_=w_grouped[:, c, j * P * PACK : (j + 1) * P * PACK],
                )

        for j in range(W_TILES):
            w_bank = acc_psum.tile([P, BLOCKS, P], F32, tag="acc")
            flip(w_rows[:, j, :], w_bank)
            target = w_grouped_words[:, :, j * P : (j + 1) * P, :]
            if j % 2 == 0:
                nc.scalar.copy(out=target, in_=by_pass(w_bank))
            else:
                nc.vector.tensor_copy(out=target, in_=by_pass(w_bank))
            if j == 1:
                spread(EMB)
            if j == 3:
                spread(GAIN1)
            if j >= 1:
                quantise_w(j - 1)
        quantise_w(W_TILES - 1)
        nc.scalar.copy(out=gain1[:], in_=gain1_bank[:])
        nc.vector.tensor_copy(out=emb_head[:], in_=emb_bank[:, :GPSIMD_COLS])

        flipped_of = {}
        grouped_of = {}
        codes_of = {}
        acc_of = {}
        sums_of = {}
        part_of = {}
        inv1_of = {}
        branch_of = {}
        resid_of = {}
        z_of = {}
        total_of = {}
        inv2_of = {}

        def transpose_tile(i):
            y_bank = flip_psum.tile([P, BLOCKS, P], F32, tag="flip")
            flip(y_tiles[i], y_bank)
            flipped_of[i] = y_bank

        def regroup_tile(i):
            grouped = operand.tile([P, D], BF16, align_bytes=64)
            nc.scalar.copy(
                out=grouped[:].bitcast(F32).rearrange("q (c r u) -> q c r u", c=PASSES, u=PAIRS),
                in_=by_pass(flipped_of[i]),
            )
            grouped_of[i] = grouped

        def quantise_tile(i):
            codes = operand.tile([P, PASSES * P], U32, align_bytes=64)
            scales = operand.tile([P, PASSES * P], U8, align_bytes=64)
            nc.vector.quantize_mx(
                out=codes[:].bitcast(FP8X4), scales=scales[:], in_=grouped_of[i][:]
            )
            codes_of[i] = (codes, scales)

        def multiply_tile(i):
            codes, scales = codes_of[i]
            banks = []
            for h in range(HALVES):
                acc = acc_psum.tile([P, BANK], F32, tag="acc")
                for c in range(PASSES):
                    nc.tensor.matmul_mx(
                        out=acc[:],
                        lhsT=codes[:, c * P : (c + 1) * P].bitcast(FP8X4),
                        lhsT_scale=scales[:, c * P : (c + 1) * P],
                        rhs=w_codes[:, c, h * BANK : (h + 1) * BANK].bitcast(FP8X4),
                        rhs_scale=w_scales[:, c, h * BANK : (h + 1) * BANK],
                        start=(c == 0),
                        stop=(c == PASSES - 1),
                    )
                banks.append(acc)
            acc_of[i] = banks

        def sum_p(i, h):
            if h == 0:
                sums = small.tile([P, HALVES], F32)
                sums_of[i] = sums
            squares = unread.tile([P, BANK], F32)
            nc.scalar.activation(
                out=squares[:], in_=acc_of[i][h][:], func=ACT.Square,
                accum_out=sums_of[i][:, h : h + 1],
            )

        def part_p(i):
            part = small.tile([P, 1], F32)
            nc.scalar.activation(
                out=part[:], in_=sums_of[i][:, 0:1], func=ACT.Identity, scale=1.0 / D,
                bias=eps_col[:],
            )
            part_of[i] = part

        def root_p(i):
            inv1 = small.tile([P, 1], F32)
            nc.scalar.activation(
                out=inv1[:], in_=sums_of[i][:, 1:2], func=ACT.Abs_reciprocal_sqrt, scale=1.0 / D,
                bias=part_of[i][:],
            )
            inv1_of[i] = inv1

        def branch_tile(i):
            branch = work.tile([P, D], F32)
            for h in range(HALVES):
                cols = slice(h * BANK, (h + 1) * BANK)
                nc.vector.scalar_tensor_tensor(
                    out=branch[:, cols], in0=acc_of[i][h][:], scalar=inv1_of[i][:],
                    in1=gain1[:, cols], op0=ALU.mult, op1=ALU.mult,
                )
            branch_of[i] = branch

        def residual_tile(i):
            resid = work.tile([P, D], F32, bufs=RESIDUAL_AHEAD + 3)
            nc.gpsimd.tensor_tensor(
                out=resid[:, :GPSIMD_COLS], in0=x_tiles[i][:, :GPSIMD_COLS], in1=emb_head[:],
                op=ALU.add,
            )
            nc.vector.tensor_tensor(
                out=resid[:, GPSIMD_COLS:], in0=x_tiles[i][:, GPSIMD_COLS:],
                in1=emb_bank[:, GPSIMD_COLS:], op=ALU.add,
            )
            resid_of[i] = resid

        def add_tile(i):
            z = work.tile([P, D], F32, bufs=FINISH_BEHIND + 2)
            engine = nc.vector if i == N_TILES - 1 else nc.gpsimd
            engine.tensor_tensor(out=z[:], in0=branch_of[i][:], in1=resid_of[i][:], op=ALU.add)
            z_of[i] = z

        def sum_z(i):
            total = small.tile([P, 1], F32)
            squares2 = unread.tile([P, D], F32, bufs=2)
            nc.scalar.activation(
                out=squares2[:], in_=z_of[i][:], func=ACT.Square, accum_out=total[:]
            )
            total_of[i] = total

        def root_z(i):
            inv2 = small.tile([P, 1], F32)
            nc.scalar.activation(
                out=inv2[:], in_=total_of[i][:], func=ACT.Abs_reciprocal_sqrt, scale=1.0 / D,
                bias=eps_col[:],
            )
            inv2_of[i] = inv2

        def finish_tile(i):
            result = work.tile([P, D], F32, bufs=4)
            nc.vector.scalar_tensor_tensor(
                out=result[:], in0=z_of[i][:], scalar=inv2_of[i][:], in1=gain2_bank[:],
                op0=ALU.mult, op1=ALU.mult,
            )
            nc.sync.dma_start(out=out_groups[i // GROUP][:, i % GROUP, :], in_=result[:])

        def live(i):
            return 0 <= i < N_TILES

        def at(stage, i, *more):
            if live(i):
                stage(i, *more)

        for s in range(-FLIP_AHEAD, N_TILES + FINISH_BEHIND):
            first_x = s + RESIDUAL_AHEAD
            if first_x % GROUP == 0 and 0 <= first_x // GROUP < N_GROUPS - LOAD_GROUPS_AHEAD:
                load_group(first_x // GROUP + LOAD_GROUPS_AHEAD, 1)
            at(branch_tile, s)
            at(add_tile, s)
            at(quantise_tile, s + QUANTISE_AHEAD)
            at(residual_tile, s + RESIDUAL_AHEAD)
            at(multiply_tile, s + MULTIPLY_AHEAD)
            if s + MULTIPLY_AHEAD == 0:
                spread(GAIN2)
            at(transpose_tile, s + FLIP_AHEAD)
            at(sum_p, s + NORM_P_AHEAD, 0)
            at(root_z, s - FINISH_BEHIND)
            at(sum_p, s + NORM_P_AHEAD, 1)
            at(part_p, s + NORM_P_AHEAD)
            at(sum_z, s - SUM_Z_BEHIND)
            at(root_p, s + NORM_P_AHEAD)
            at(regroup_tile, s + REGROUP_AHEAD)
            at(finish_tile, s - FINISH_BEHIND)
